import numpy as np
import ml_dtypes


def mxq(x, axis, fmt="e4m3"):
    dtype, down = {"e4m3": (ml_dtypes.float8_e4m3fn, 7), "e5m2": (ml_dtypes.float8_e5m2, 14)}[fmt]
    v = np.moveaxis(np.asarray(x, np.float32).astype(ml_dtypes.bfloat16).astype(np.float64), axis, -1)
    blocks = v.reshape(v.shape[:-1] + (-1, 32))
    amax = np.abs(blocks).max(-1, keepdims=True)
    byte = np.maximum(np.where(amax > 0, np.frexp(amax)[1] - 1 + 127, 0) - down, 1)
    scale = np.exp2(byte - 127.0)
    codes = (blocks / scale).astype(np.float32).astype(dtype).astype(np.float64)
    return np.moveaxis((codes * scale).reshape(v.shape), -1, axis)


WIDE = False


def mx_kscale(k):
    if not WIDE:
        return np.ones(k)
    levels = np.array([10, -10, 5, -5, 0])
    if k % 512:
        return np.exp2(np.random.permutation(np.resize(levels, k // 32))).repeat(32)
    a = np.empty((k // 512, 16))
    for p in range(k // 512):
        a[p, :8] = np.random.permutation(np.resize(levels, 8))
        for g in range(8):
            far = levels[np.abs(levels - a[p, g]) >= 10]
            a[p, g + 8] = far[np.random.randint(len(far))]
    return np.exp2(a.ravel()).repeat(32)


BF16 = ml_dtypes.bfloat16


def bf(x):
    return np.asarray(x, np.float32).astype(BF16)


def f64(x):
    return np.asarray(x).astype(np.float64)


B, T, D, NH, N_MLP = 4, 1024, 512, 8, 4096
HD = D // NH
LN_EPS = 1e-6


def layer_norm(v, g, b):
    mu = v.mean(-1, keepdims=True)
    var = np.square(v - mu).mean(-1, keepdims=True)
    return (v - mu) / np.sqrt(var + LN_EPS) * g + b


def setup_inputs():
    s = mx_kscale(D)
    return {"x": bf(np.random.standard_normal((B, T, D)) * 1.5 + np.random.standard_normal((B, T, 1)) * 0.5),
            "W_qkv": bf(np.random.standard_normal((3 * D, D)) / np.sqrt(D) / s),
            "b_qkv": bf(np.random.standard_normal(3 * D) * 0.2),
            "g1": bf((1.0 + 0.1 * np.random.standard_normal(D)) * s),
            "beta1": bf(0.1 * np.random.standard_normal(D) * s)}


def reference(x, W_qkv, b_qkv, g1, beta1):
    h = layer_norm(f64(x), f64(g1), f64(beta1))
    qkv = (mxq(h, 2, "e4m3") @ mxq(f64(W_qkv), 1, "e4m3").T) + f64(b_qkv)
    qkv = qkv.reshape(B, T, 3, NH, HD)
    return qkv[:, :, 0].copy(), qkv[:, :, 1].copy(), qkv[:, :, 2].copy()

@@ -1,0 +1,301 @@
+from contextlib import ExitStack
+
+import concourse.mybir as mybir
+from concourse.masks import make_identity
+
+F32 = mybir.dt.float32
+BF16 = mybir.dt.bfloat16
+U32 = mybir.dt.uint32
+U8 = mybir.dt.uint8
+FP8X4 = mybir.dt.float8_e4m3fn_x4
+ACT = mybir.ActivationFunctionType
+ALU = mybir.AluOpType
+
+P = 128
+PACK = 4
+HALVES = 2
+D = P * PACK
+TOKENS = 4 * 1024
+OUTS = 3
+ROWS = 4
+GROUP = P * ROWS
+N_GROUPS = TOKENS // GROUP
+N_ROWS = N_GROUPS * ROWS
+W_TILES = OUTS * D // P
+LN_EPS = 1e-6
+STORE_ROWS = 2
+
+LAG_RSTD = ROWS
+LAG_XHAT = LAG_RSTD + 1
+LAG_TURN = LAG_XHAT + ROWS
+LAG_PLANE_OUT = LAG_TURN + 1
+LAG_REGROUP = LAG_PLANE_OUT + PACK - 1
+LAG_QUANTISE = LAG_REGROUP + 1
+LAG_MATMUL = LAG_QUANTISE + 1
+LAG_BIAS = LAG_MATMUL + 1
+N_STEPS = N_ROWS + LAG_BIAS
+
+FLOPS = 2 * TOKENS * D * OUTS * D
+
+
+def tile_block_pa_t_kernel(tc, x, W_qkv, b_qkv, g1, beta1, out_0, out_1, out_2):
+    nc = tc.nc
+
+    x_groups = x.flatten_outer_dims().rearrange("(s p i) k -> s p i k", p=P, i=ROWS)
+    out_groups = [
+        out.rearrange("b t h d -> (b t) (h d)").rearrange("(s p i) f -> s p i f", p=P, i=ROWS)
+        for out in (out_0, out_1, out_2)
+    ]
+    w_rows = W_qkv.rearrange("(r p) k -> p r k", p=P)
+
+    with ExitStack() as ctx:
+        consts = ctx.enter_context(tc.tile_pool(name="consts", bufs=1))
+        x_pool = ctx.enter_context(tc.tile_pool(name="x_pool", bufs=N_GROUPS))
+        small = ctx.enter_context(tc.tile_pool(name="small", bufs=4))
+        xhat_pool = ctx.enter_context(tc.tile_pool(name="xhat_pool", bufs=3))
+        plane_pool = ctx.enter_context(tc.tile_pool(name="plane_pool", bufs=3))
+        row_pool = ctx.enter_context(tc.tile_pool(name="row_pool", bufs=2 * ROWS))
+        stage_pool = ctx.enter_context(tc.tile_pool(name="stage_pool", bufs=3))
+        turn_psum = ctx.enter_context(tc.psum_pool(name="turn_psum", bufs=2))
+        acc_psum = ctx.enter_context(tc.psum_pool(name="acc_psum", bufs=2))
+        ctx.enter_context(tc.manual_schedule())
+
+        x_tiles = []
+        for s in range(N_GROUPS):
+            x_tiles.append(x_pool.tile([P, ROWS, D], BF16, name="x_grp", tag="x_grp"))
+        w_sb = consts.tile([P, W_TILES, D], BF16)
+        g1_in = consts.tile([P, PACK], BF16)
+        beta1_in = consts.tile([P, PACK], BF16)
+        bias = consts.tile([P, OUTS, D], BF16)
+
+        def load_weights(o):
+            tiles_of_o = slice(o * PACK, (o + 1) * PACK)
+            nc.sync.dma_start(out=w_sb[:, tiles_of_o, :], in_=w_rows[:, tiles_of_o, :])
+
+        nc.sync.dma_start(out=x_tiles[0][:], in_=x_groups[0])
+        load_weights(0)
+        nc.sync.dma_start(out=x_tiles[1][:], in_=x_groups[1])
+        load_weights(1)
+        load_weights(2)
+        nc.sync.dma_start(out=g1_in[:], in_=g1.rearrange("(p t) -> p t", t=PACK))
+        nc.sync.dma_start(out=beta1_in[:], in_=beta1.rearrange("(p t) -> p t", t=PACK))
+        nc.sync.dma_start(out=x_tiles[2][:], in_=x_groups[2])
+        nc.sync.dma_start(out=x_tiles[3][:], in_=x_groups[3])
+        nc.sync.dma_start(out=bias[:].rearrange("p o f -> p (o f)"), in_=b_qkv.partition_broadcast(P))
+        for s in range(4, N_GROUPS):
+            nc.sync.dma_start(out=x_tiles[s][:], in_=x_groups[s])
+
+        ident_f32 = consts.tile([P, P], F32)
+        make_identity(nc, ident_f32[:])
+        eps = consts.tile([P, 1], F32)
+        nc.vector.memset(eps[:], LN_EPS)
+        warm = consts.tile([P, 1], F32)
+        nc.scalar.activation(out=warm[:], in_=eps[:], func=ACT.Sqrt)
+
+        affine = consts.tile([P, 2 * PACK], F32)
+
+        def widen_affine():
+            nc.vector.tensor_copy(out=affine[:, 0:PACK], in_=g1_in[:])
+            nc.vector.tensor_copy(out=affine[:, PACK : 2 * PACK], in_=beta1_in[:])
+
+        w_words = w_sb[:].bitcast(F32)
+        w_grouped = consts.tile([P, OUTS * D, PACK], BF16, align_bytes=64)
+        w_grouped_words = w_grouped[:].bitcast(F32)
+        w_codes = consts.tile([P, OUTS * D], U32, align_bytes=64)
+        w_scales = consts.tile([P, OUTS * D], U8, align_bytes=64)
+
+        def turn_weight_tile(r):
+            w_turned = acc_psum.tile([P, HALVES, P], F32, tag="acc_%d" % (r % OUTS))
+            for u in range(HALVES):
+                nc.tensor.transpose(w_turned[:, u, :], w_words[:, r, u::HALVES], ident_f32[:])
+            dst = w_grouped_words[:, r * P : (r + 1) * P, :]
+            src = w_turned[:].rearrange("p u f -> p f u")
+            if r < PACK:
+                nc.scalar.copy(out=dst, in_=src)
+            else:
+                nc.vector.tensor_copy(out=dst, in_=src)
+
+        def quantise_weights(o):
+            cols = slice(o * D, (o + 1) * D)
+            nc.vector.quantize_mx(
+                out=w_codes[:, cols].bitcast(FP8X4),
+                scales=w_scales[:, cols],
+                in_=w_grouped[:, cols, :].rearrange("p f t -> p (f t)"),
+            )
+
+        stats_of = {}
+        mean_var_of = {}
+        std_of = {}
+        rstd_of = {}
+        shift_of = {}
+        xhat_of = {}
+        turned_of = {}
+        planes_of = {}
+        grouped_of = {}
+        codes_of = {}
+        scales_of = {}
+        accs_of = {}
+        stage_of = {}
+
+        def statistics(s, i):
+            if i == 0:
+                stats_of[s] = small.tile([P, ROWS, 6], F32, name="stats")
+            nc.vector.bn_stats(out=stats_of[s][:, i, :], in_=x_tiles[s][:, i, :])
+
+        def mean_and_std(s):
+            mean_var = small.tile([P, ROWS, 2], F32)
+            for i in range(ROWS):
+                nc.vector.bn_aggr(out=mean_var[:, i, :], in_=stats_of[s][:, i, :])
+            std = small.tile([P, ROWS], F32)
+            nc.scalar.activation(out=std[:], in_=mean_var[:, :, 1], func=ACT.Sqrt, bias=eps[:, 0:1], scale=1.0)
+            mean_var_of[s] = mean_var
+            std_of[s] = std
+
+        def reciprocal_std(s):
+            rstd_of[s] = small.tile([P, ROWS], F32, name="rstd")
+            nc.vector.reciprocal(out=rstd_of[s][:], in_=std_of[s][:])
+
+        def shift(s):
+            shift_of[s] = small.tile([P, ROWS], F32, name="shift")
+            nc.vector.scalar_tensor_tensor(
+                out=shift_of[s][:],
+                in0=mean_var_of[s][:, :, 0],
+                scalar=-1.0,
+                in1=rstd_of[s][:],
+                op0=ALU.mult,
+                op1=ALU.mult,
+            )
+
+        def normalise_row(s, i):
+            if i == 0:
+                xhat_of[s] = xhat_pool.tile([P, ROWS, D], F32, name="xhat")
+            dst = xhat_of[s][:, i, :].rearrange("p (t q) -> p t q", t=PACK)
+            src = x_tiles[s][:, i, :].rearrange("p (q t) -> p t q", t=PACK)
+            if i % 2 == 0:
+                nc.scalar.activation(
+                    out=dst,
+                    in_=src,
+                    func=ACT.Identity,
+                    scale=rstd_of[s][:, i : i + 1],
+                    bias=shift_of[s][:, i : i + 1],
+                )
+            else:
+                nc.gpsimd.tensor_scalar(
+                    out=dst,
+                    in0=src,
+                    scalar1=rstd_of[s][:, i : i + 1],
+                    scalar2=shift_of[s][:, i : i + 1],
+                    op0=ALU.mult,
+                    op1=ALU.add,
+                )
+
+        def turn_plane(s, t):
+            plane = turn_psum.tile([P, GROUP], F32, tag="turn")
+            for i in range(ROWS):
+                nc.tensor.transpose(
+                    plane[:, i * P : (i + 1) * P], xhat_of[s][:, i, t * P : (t + 1) * P], ident_f32[:]
+                )
+            turned_of[s, t] = plane
+
+        def plane_out(s, t):
+            if t == 0:
+                planes_of[s] = plane_pool.tile([P, PACK, GROUP], BF16, name="planes")
+            nc.scalar.activation(
+                out=planes_of[s][:, t, :],
+                in_=turned_of[s, t][:],
+                func=ACT.Identity,
+                scale=affine[:, t : t + 1],
+                bias=affine[:, PACK + t : PACK + t + 1],
+            )
+
+        def regroup_row(s, i):
+            grouped = row_pool.tile([P, P, PACK], BF16, align_bytes=64)
+            nc.scalar.copy(
+                out=grouped[:].rearrange("p (c j) t -> p c t j", j=4),
+                in_=planes_of[s][:, :, i * P : (i + 1) * P].rearrange("p t (c j) -> p c t j", j=4),
+            )
+            grouped_of[s, i] = grouped
+
+        def quantise_row(s, i):
+            codes = row_pool.tile([P, P], U32, align_bytes=64)
+            scales = row_pool.tile([P, P], U8, align_bytes=64)
+            nc.vector.quantize_mx(
+                out=codes[:].bitcast(FP8X4),
+                scales=scales[:],
+                in_=grouped_of[s, i][:].rearrange("p c t -> p (c t)"),
+            )
+            codes_of[s, i] = codes
+            scales_of[s, i] = scales
+
+        def matmul_row(s, i):
+            accs = []
+            for o in range(OUTS):
+                acc = acc_psum.tile([P, D], F32, name="acc_%d" % o)
+                nc.tensor.matmul_mx(
+                    out=acc[:],
+                    lhsT=codes_of[s, i][:].bitcast(FP8X4),
+                    lhsT_scale=scales_of[s, i][:],
+                    rhs=w_codes[:, o * D : (o + 1) * D].bitcast(FP8X4),
+                    rhs_scale=w_scales[:, o * D : (o + 1) * D],
+                    start=True,
+                    stop=True,
+                )
+                accs.append(acc)
+            accs_of[s, i] = accs
+
+        def bias_row(s, i):
+            if i == 0:
+                stage_of[s] = [
+                    stage_pool.tile([P, ROWS, D], F32, name="stage_%d" % o) for o in range(OUTS)
+                ]
+            accs = accs_of[s, i]
+            for o in range(OUTS):
+                dst = stage_of[s][o][:, i, :]
+                if o < OUTS - 1:
+                    nc.vector.tensor_tensor(out=dst, in0=accs[o][:], in1=bias[:, o, :], op=ALU.add)
+                else:
+                    nc.scalar.copy(out=dst, in_=accs[o][:])
+                    nc.gpsimd.tensor_tensor(out=dst, in0=dst, in1=bias[:, o, :], op=ALU.add)
+            if (i + 1) % STORE_ROWS == 0:
+                done = slice(i + 1 - STORE_ROWS, i + 1)
+                for o in range(OUTS):
+                    nc.sync.dma_start(out=out_groups[o][s][:, done, :], in_=stage_of[s][o][:, done, :])
+
+        for step in range(N_STEPS):
+            n = step - LAG_RSTD
+            group_is_counted = n % ROWS == 0 and 0 <= n < N_ROWS
+            if group_is_counted:
+                mean_and_std(n // ROWS)
+            if step < N_ROWS:
+                statistics(step // ROWS, step % ROWS)
+            if group_is_counted:
+                reciprocal_std(n // ROWS)
+            n = step - LAG_XHAT
+            if 0 <= n < N_ROWS:
+                normalise_row(n // ROWS, n % ROWS)
+            if step < W_TILES:
+                turn_weight_tile(step)
+            elif step < W_TILES + OUTS:
+                quantise_weights(step - W_TILES)
+            if step == LAG_TURN - 1:
+                widen_affine()
+            n = step - LAG_TURN
+            if 0 <= n < N_ROWS:
+                turn_plane(n // PACK, n % PACK)
+            n = step - LAG_PLANE_OUT
+            if 0 <= n < N_ROWS:
+                plane_out(n // PACK, n % PACK)
+            n = step - LAG_MATMUL
+            if 0 <= n < N_ROWS:
+                matmul_row(n // ROWS, n % ROWS)
+            n = step - LAG_BIAS
+            if 0 <= n < N_ROWS:
+                bias_row(n // ROWS, n % ROWS)
+            if group_is_counted:
+                shift((step - LAG_RSTD) // ROWS)
+            n = step - LAG_REGROUP
+            if 0 <= n < N_ROWS:
+                regroup_row(n // ROWS, n % ROWS)
+            n = step - LAG_QUANTISE
+            if 0 <= n < N_ROWS:
+                quantise_row(n // ROWS, n % ROWS)

@@ -22,18 +22,28 @@ GROUP = P * ROWS
 N_GROUPS = TOKENS // GROUP
 N_ROWS = N_GROUPS * ROWS
 W_TILES = OUTS * D // P
+W_STEP_TILES = 2
+W_QUANTISE_STEP = 7
+W_FIRST_STEP = 2
 LN_EPS = 1e-6
+VECTOR_LAST_ROWS = 2
 STORE_ROWS = 2
 
 LAG_RSTD = ROWS
 LAG_XHAT = LAG_RSTD + 1
-LAG_TURN = LAG_XHAT + ROWS
+XHAT_ROWS = 2
+LAG_TURN = LAG_XHAT + ROWS // XHAT_ROWS
 LAG_PLANE_OUT = LAG_TURN + 1
 LAG_REGROUP = LAG_PLANE_OUT + PACK - 1
 LAG_QUANTISE = LAG_REGROUP + 1
 LAG_MATMUL = LAG_QUANTISE + 1
 LAG_BIAS = LAG_MATMUL + 1
 N_STEPS = N_ROWS + LAG_BIAS
+
+XHAT_ENGINES = (
+    ("gpsimd", "gpsimd", "scalar", "vector"),
+    ("gpsimd", "vector", "gpsimd", "scalar"),
+)
 
 FLOPS = 2 * TOKENS * D * OUTS * D
 
@@ -72,7 +82,8 @@ def tile_block_pa_t_kernel(tc, x, W_qkv, b_qkv, g1, beta1, out_0, out_1, out_2):
             tiles_of_o = slice(o * PACK, (o + 1) * PACK)
             nc.sync.dma_start(out=w_sb[:, tiles_of_o, :], in_=w_rows[:, tiles_of_o, :])
 
-        nc.sync.dma_start(out=x_tiles[0][:], in_=x_groups[0])
+        for half in (slice(0, ROWS // 2), slice(ROWS // 2, ROWS)):
+            nc.sync.dma_start(out=x_tiles[0][:, half, :], in_=x_groups[0][:, half, :])
         load_weights(0)
         nc.sync.dma_start(out=x_tiles[1][:], in_=x_groups[1])
         load_weights(1)
@@ -80,9 +91,8 @@ def tile_block_pa_t_kernel(tc, x, W_qkv, b_qkv, g1, beta1, out_0, out_1, out_2):
         nc.sync.dma_start(out=g1_in[:], in_=g1.rearrange("(p t) -> p t", t=PACK))
         nc.sync.dma_start(out=beta1_in[:], in_=beta1.rearrange("(p t) -> p t", t=PACK))
         nc.sync.dma_start(out=x_tiles[2][:], in_=x_groups[2])
-        nc.sync.dma_start(out=x_tiles[3][:], in_=x_groups[3])
         nc.sync.dma_start(out=bias[:].rearrange("p o f -> p (o f)"), in_=b_qkv.partition_broadcast(P))
-        for s in range(4, N_GROUPS):
+        for s in range(3, N_GROUPS):
             nc.sync.dma_start(out=x_tiles[s][:], in_=x_groups[s])
 
         ident_f32 = consts.tile([P, P], F32)
@@ -90,7 +100,7 @@ def tile_block_pa_t_kernel(tc, x, W_qkv, b_qkv, g1, beta1, out_0, out_1, out_2):
         eps = consts.tile([P, 1], F32)
         nc.vector.memset(eps[:], LN_EPS)
         warm = consts.tile([P, 1], F32)
-        nc.scalar.activation(out=warm[:], in_=eps[:], func=ACT.Sqrt)
+        nc.scalar.activation(out=warm[:], in_=eps[:], func=ACT.Abs_reciprocal_sqrt)
 
         affine = consts.tile([P, 2 * PACK], F32)
 
@@ -108,12 +118,9 @@ def tile_block_pa_t_kernel(tc, x, W_qkv, b_qkv, g1, beta1, out_0, out_1, out_2):
             w_turned = acc_psum.tile([P, HALVES, P], F32, tag="acc_%d" % (r % OUTS))
             for u in range(HALVES):
                 nc.tensor.transpose(w_turned[:, u, :], w_words[:, r, u::HALVES], ident_f32[:])
-            dst = w_grouped_words[:, r * P : (r + 1) * P, :]
-            src = w_turned[:].rearrange("p u f -> p f u")
-            if r < PACK:
-                nc.scalar.copy(out=dst, in_=src)
-            else:
-                nc.vector.tensor_copy(out=dst, in_=src)
+            nc.scalar.copy(
+                out=w_grouped_words[:, r * P : (r + 1) * P, :], in_=w_turned[:].rearrange("p u f -> p f u")
+            )
 
         def quantise_weights(o):
             cols = slice(o * D, (o + 1) * D)
@@ -125,7 +132,6 @@ def tile_block_pa_t_kernel(tc, x, W_qkv, b_qkv, g1, beta1, out_0, out_1, out_2):
 
         stats_of = {}
         mean_var_of = {}
-        std_of = {}
         rstd_of = {}
         shift_of = {}
         xhat_of = {}
@@ -142,18 +148,16 @@ def tile_block_pa_t_kernel(tc, x, W_qkv, b_qkv, g1, beta1, out_0, out_1, out_2):
                 stats_of[s] = small.tile([P, ROWS, 6], F32, name="stats")
             nc.vector.bn_stats(out=stats_of[s][:, i, :], in_=x_tiles[s][:, i, :])
 
-        def mean_and_std(s):
+        def mean_and_rstd(s):
             mean_var = small.tile([P, ROWS, 2], F32)
             for i in range(ROWS):
                 nc.vector.bn_aggr(out=mean_var[:, i, :], in_=stats_of[s][:, i, :])
-            std = small.tile([P, ROWS], F32)
-            nc.scalar.activation(out=std[:], in_=mean_var[:, :, 1], func=ACT.Sqrt, bias=eps[:, 0:1], scale=1.0)
+            rstd = small.tile([P, ROWS], F32)
+            nc.scalar.activation(
+                out=rstd[:], in_=mean_var[:, :, 1], func=ACT.Abs_reciprocal_sqrt, bias=eps[:, 0:1], scale=1.0
+            )
             mean_var_of[s] = mean_var
-            std_of[s] = std
-
-        def reciprocal_std(s):
-            rstd_of[s] = small.tile([P, ROWS], F32, name="rstd")
-            nc.vector.reciprocal(out=rstd_of[s][:], in_=std_of[s][:])
+            rstd_of[s] = rstd
 
         def shift(s):
             shift_of[s] = small.tile([P, ROWS], F32, name="shift")
@@ -171,7 +175,8 @@ def tile_block_pa_t_kernel(tc, x, W_qkv, b_qkv, g1, beta1, out_0, out_1, out_2):
                 xhat_of[s] = xhat_pool.tile([P, ROWS, D], F32, name="xhat")
             dst = xhat_of[s][:, i, :].rearrange("p (t q) -> p t q", t=PACK)
             src = x_tiles[s][:, i, :].rearrange("p (q t) -> p t q", t=PACK)
-            if i % 2 == 0:
+            engine = XHAT_ENGINES[0 if s == 0 else 1][i]
+            if engine == "scalar":
                 nc.scalar.activation(
                     out=dst,
                     in_=src,
@@ -180,7 +185,7 @@ def tile_block_pa_t_kernel(tc, x, W_qkv, b_qkv, g1, beta1, out_0, out_1, out_2):
                     bias=shift_of[s][:, i : i + 1],
                 )
             else:
-                nc.gpsimd.tensor_scalar(
+                (nc.vector if engine == "vector" else nc.gpsimd).tensor_scalar(
                     out=dst,
                     in0=src,
                     scalar1=rstd_of[s][:, i : i + 1],
@@ -251,13 +256,14 @@ def tile_block_pa_t_kernel(tc, x, W_qkv, b_qkv, g1, beta1, out_0, out_1, out_2):
             accs = accs_of[s, i]
             for o in range(OUTS):
                 dst = stage_of[s][o][:, i, :]
-                if o < OUTS - 1:
+                if o < OUTS - 1 or s * ROWS + i >= N_ROWS - VECTOR_LAST_ROWS:
                     nc.vector.tensor_tensor(out=dst, in0=accs[o][:], in1=bias[:, o, :], op=ALU.add)
                 else:
                     nc.scalar.copy(out=dst, in_=accs[o][:])
                     nc.gpsimd.tensor_tensor(out=dst, in0=dst, in1=bias[:, o, :], op=ALU.add)
-            if (i + 1) % STORE_ROWS == 0:
-                done = slice(i + 1 - STORE_ROWS, i + 1)
+            store_rows = STORE_ROWS if s < N_GROUPS - 1 else 1
+            if (i + 1) % store_rows == 0:
+                done = slice(i + 1 - store_rows, i + 1)
                 for o in range(OUTS):
                     nc.sync.dma_start(out=out_groups[o][s][:, done, :], in_=stage_of[s][o][:, done, :])
 
@@ -265,18 +271,26 @@ def tile_block_pa_t_kernel(tc, x, W_qkv, b_qkv, g1, beta1, out_0, out_1, out_2):
             n = step - LAG_RSTD
             group_is_counted = n % ROWS == 0 and 0 <= n < N_ROWS
             if group_is_counted:
-                mean_and_std(n // ROWS)
+                mean_and_rstd(n // ROWS)
+            n = step - LAG_MATMUL
+            if 0 <= n < N_ROWS:
+                matmul_row(n // ROWS, n % ROWS)
+            w = (step - W_FIRST_STEP) * W_STEP_TILES
+            if 0 <= w < W_TILES:
+                for r in range(w, w + W_STEP_TILES):
+                    turn_weight_tile(r)
+            n = step - LAG_XHAT
+            if 0 <= n < N_ROWS and n % ROWS < ROWS // XHAT_ROWS:
+                for i in range(n % ROWS * XHAT_ROWS, (n % ROWS + 1) * XHAT_ROWS):
+                    normalise_row(n // ROWS, i)
+            o = step - W_QUANTISE_STEP
+            if 0 <= o < OUTS:
+                quantise_weights(o)
+            n = step - LAG_BIAS
+            if 0 <= n < N_ROWS:
+                bias_row(n // ROWS, n % ROWS)
             if step < N_ROWS:
                 statistics(step // ROWS, step % ROWS)
-            if group_is_counted:
-                reciprocal_std(n // ROWS)
-            n = step - LAG_XHAT
-            if 0 <= n < N_ROWS:
-                normalise_row(n // ROWS, n % ROWS)
-            if step < W_TILES:
-                turn_weight_tile(step)
-            elif step < W_TILES + OUTS:
-                quantise_weights(step - W_TILES)
             if step == LAG_TURN - 1:
                 widen_affine()
             n = step - LAG_TURN
@@ -285,17 +299,11 @@ def tile_block_pa_t_kernel(tc, x, W_qkv, b_qkv, g1, beta1, out_0, out_1, out_2):
             n = step - LAG_PLANE_OUT
             if 0 <= n < N_ROWS:
                 plane_out(n // PACK, n % PACK)
-            n = step - LAG_MATMUL
-            if 0 <= n < N_ROWS:
-                matmul_row(n // ROWS, n % ROWS)
-            n = step - LAG_BIAS
-            if 0 <= n < N_ROWS:
-                bias_row(n // ROWS, n % ROWS)
             if group_is_counted:
                 shift((step - LAG_RSTD) // ROWS)
-            n = step - LAG_REGROUP
-            if 0 <= n < N_ROWS:
-                regroup_row(n // ROWS, n % ROWS)
             n = step - LAG_QUANTISE
             if 0 <= n < N_ROWS:
                 quantise_row(n // ROWS, n % ROWS)
+            n = step - LAG_REGROUP
+            if 0 <= n < N_ROWS:
+                regroup_row(n // ROWS, n % ROWS)

@@ -41,8 +41,8 @@ LAG_BIAS = LAG_MATMUL + 1
 N_STEPS = N_ROWS + LAG_BIAS
 
 XHAT_ENGINES = (
-    ("gpsimd", "gpsimd", "scalar", "vector"),
-    ("gpsimd", "vector", "gpsimd", "scalar"),
+    ("gpsimd", "gpsimd", "scalar", "scalar"),
+    ("gpsimd", "scalar", "gpsimd", "scalar"),
 )
 
 FLOPS = 2 * TOKENS * D * OUTS * D
@@ -185,7 +185,7 @@ def tile_block_pa_t_kernel(tc, x, W_qkv, b_qkv, g1, beta1, out_0, out_1, out_2):
                     bias=shift_of[s][:, i : i + 1],
                 )
             else:
-                (nc.vector if engine == "vector" else nc.gpsimd).tensor_scalar(
+                nc.gpsimd.tensor_scalar(
                     out=dst,
                     in0=src,
                     scalar1=rstd_of[s][:, i : i + 1],

@@ -26,8 +26,6 @@ W_STEP_TILES = 2
 W_QUANTISE_STEP = 7
 W_FIRST_STEP = 2
 LN_EPS = 1e-6
-VECTOR_LAST_ROWS = 2
-STORE_ROWS = 2
 
 LAG_RSTD = ROWS
 LAG_XHAT = LAG_RSTD + 1
@@ -39,10 +37,11 @@ LAG_QUANTISE = LAG_REGROUP + 1
 LAG_MATMUL = LAG_QUANTISE + 1
 LAG_BIAS = LAG_MATMUL + 1
 N_STEPS = N_ROWS + LAG_BIAS
+FIRST_ROW_AFTER_STATISTICS = N_ROWS - LAG_BIAS
 
 XHAT_ENGINES = (
-    ("gpsimd", "gpsimd", "scalar", "scalar"),
-    ("gpsimd", "scalar", "gpsimd", "scalar"),
+    ("gpsimd", "gpsimd", "gpsimd", "scalar"),
+    ("gpsimd", "gpsimd", "scalar", "gpsimd"),
 )
 
 FLOPS = 2 * TOKENS * D * OUTS * D
@@ -254,18 +253,18 @@ def tile_block_pa_t_kernel(tc, x, W_qkv, b_qkv, g1, beta1, out_0, out_1, out_2):
                     stage_pool.tile([P, ROWS, D], F32, name="stage_%d" % o) for o in range(OUTS)
                 ]
             accs = accs_of[s, i]
+            row = s * ROWS + i
+            after = row - FIRST_ROW_AFTER_STATISTICS
+            vector_takes_v = (after >= 0 and after % 2 == 0) or row == N_ROWS - 1
             for o in range(OUTS):
                 dst = stage_of[s][o][:, i, :]
-                if o < OUTS - 1 or s * ROWS + i >= N_ROWS - VECTOR_LAST_ROWS:
+                if o < OUTS - 1 or vector_takes_v:
                     nc.vector.tensor_tensor(out=dst, in0=accs[o][:], in1=bias[:, o, :], op=ALU.add)
                 else:
                     nc.scalar.copy(out=dst, in_=accs[o][:])
                     nc.gpsimd.tensor_tensor(out=dst, in0=dst, in1=bias[:, o, :], op=ALU.add)
-            store_rows = STORE_ROWS if s < N_GROUPS - 1 else 1
-            if (i + 1) % store_rows == 0:
-                done = slice(i + 1 - store_rows, i + 1)
-                for o in range(OUTS):
-                    nc.sync.dma_start(out=out_groups[o][s][:, done, :], in_=stage_of[s][o][:, done, :])
+            for o in range(OUTS):
+                nc.sync.dma_start(out=out_groups[o][s][:, i, :], in_=stage_of[s][o][:, i, :])
 
         for step in range(N_STEPS):
             n = step - LAG_RSTD

@@ -37,6 +37,7 @@ LAG_QUANTISE = LAG_REGROUP + 1
 LAG_MATMUL = LAG_QUANTISE + 1
 LAG_BIAS = LAG_MATMUL + 1
 N_STEPS = N_ROWS + LAG_BIAS
+STORE_ROWS = 2
 FIRST_ROW_AFTER_STATISTICS = N_ROWS - LAG_BIAS
 
 XHAT_ENGINES = (
@@ -263,8 +264,11 @@ def tile_block_pa_t_kernel(tc, x, W_qkv, b_qkv, g1, beta1, out_0, out_1, out_2):
                 else:
                     nc.scalar.copy(out=dst, in_=accs[o][:])
                     nc.gpsimd.tensor_tensor(out=dst, in0=dst, in1=bias[:, o, :], op=ALU.add)
-            for o in range(OUTS):
-                nc.sync.dma_start(out=out_groups[o][s][:, i, :], in_=stage_of[s][o][:, i, :])
+            store_rows = STORE_ROWS if s < N_GROUPS - 1 else 1
+            if (i + 1) % store_rows == 0:
+                done = slice(i + 1 - store_rows, i + 1)
+                for o in range(OUTS):
+                    nc.sync.dma_start(out=out_groups[o][s][:, done, :], in_=stage_of[s][o][:, done, :])
 
         for step in range(N_STEPS):
             n = step - LAG_RSTD

@@ -41,8 +41,8 @@ STORE_ROWS = 2
 FIRST_ROW_AFTER_STATISTICS = N_ROWS - LAG_BIAS
 
 XHAT_ENGINES = (
-    ("gpsimd", "gpsimd", "gpsimd", "scalar"),
-    ("gpsimd", "gpsimd", "scalar", "gpsimd"),
+    ("gpsimd", "gpsimd", "scalar", "scalar"),
+    ("gpsimd", "scalar", "gpsimd", "scalar"),
 )
 
 FLOPS = 2 * TOKENS * D * OUTS * D

@@ -264,9 +264,8 @@ def tile_block_pa_t_kernel(tc, x, W_qkv, b_qkv, g1, beta1, out_0, out_1, out_2):
                 else:
                     nc.scalar.copy(out=dst, in_=accs[o][:])
                     nc.gpsimd.tensor_tensor(out=dst, in0=dst, in1=bias[:, o, :], op=ALU.add)
-            store_rows = STORE_ROWS if s < N_GROUPS - 1 else 1
-            if (i + 1) % store_rows == 0:
-                done = slice(i + 1 - store_rows, i + 1)
+            if (i + 1) % STORE_ROWS == 0:
+                done = slice(i + 1 - STORE_ROWS, i + 1)
                 for o in range(OUTS):
                     nc.sync.dma_start(out=out_groups[o][s][:, done, :], in_=stage_of[s][o][:, done, :])
 
@@ -278,10 +277,6 @@ def tile_block_pa_t_kernel(tc, x, W_qkv, b_qkv, g1, beta1, out_0, out_1, out_2):
             n = step - LAG_MATMUL
             if 0 <= n < N_ROWS:
                 matmul_row(n // ROWS, n % ROWS)
-            w = (step - W_FIRST_STEP) * W_STEP_TILES
-            if 0 <= w < W_TILES:
-                for r in range(w, w + W_STEP_TILES):
-                    turn_weight_tile(r)
             n = step - LAG_XHAT
             if 0 <= n < N_ROWS and n % ROWS < ROWS // XHAT_ROWS:
                 for i in range(n % ROWS * XHAT_ROWS, (n % ROWS + 1) * XHAT_ROWS):
@@ -294,6 +289,10 @@ def tile_block_pa_t_kernel(tc, x, W_qkv, b_qkv, g1, beta1, out_0, out_1, out_2):
                 bias_row(n // ROWS, n % ROWS)
             if step < N_ROWS:
                 statistics(step // ROWS, step % ROWS)
+            w = (step - W_FIRST_STEP) * W_STEP_TILES
+            if 0 <= w < W_TILES:
+                for r in range(w, w + W_STEP_TILES):
+                    turn_weight_tile(r)
             if step == LAG_TURN - 1:
                 widen_affine()
             n = step - LAG_TURN

@@ -18,32 +18,29 @@ D = P * PACK
 TOKENS = 4 * 1024
 OUTS = 3
 ROWS = 4
+PAIR = 2
 GROUP = P * ROWS
 N_GROUPS = TOKENS // GROUP
 N_ROWS = N_GROUPS * ROWS
 W_TILES = OUTS * D // P
 W_STEP_TILES = 2
-W_QUANTISE_STEP = 7
 W_FIRST_STEP = 2
+W_QUANTISE_STEP = 6
 LN_EPS = 1e-6
 
-LAG_RSTD = ROWS
+LAG_RSTD = PAIR
 LAG_XHAT = LAG_RSTD + 1
-XHAT_ROWS = 2
-LAG_TURN = LAG_XHAT + ROWS // XHAT_ROWS
+LAG_TURN = LAG_XHAT + PAIR
+STEP_PLANES = PACK // PAIR
 LAG_PLANE_OUT = LAG_TURN + 1
-LAG_REGROUP = LAG_PLANE_OUT + PACK - 1
+LAG_REGROUP = LAG_PLANE_OUT + PAIR - 1
 LAG_QUANTISE = LAG_REGROUP + 1
 LAG_MATMUL = LAG_QUANTISE + 1
 LAG_BIAS = LAG_MATMUL + 1
 N_STEPS = N_ROWS + LAG_BIAS
 STORE_ROWS = 2
-FIRST_ROW_AFTER_STATISTICS = N_ROWS - LAG_BIAS
-
-XHAT_ENGINES = (
-    ("gpsimd", "gpsimd", "scalar", "scalar"),
-    ("gpsimd", "scalar", "gpsimd", "scalar"),
-)
+XHAT_CYCLE = 8
+VECTOR_V_ROWS = 5
 
 FLOPS = 2 * TOKENS * D * OUTS * D
 
@@ -61,9 +58,9 @@ def tile_block_pa_t_kernel(tc, x, W_qkv, b_qkv, g1, beta1, out_0, out_1, out_2):
     with ExitStack() as ctx:
         consts = ctx.enter_context(tc.tile_pool(name="consts", bufs=1))
         x_pool = ctx.enter_context(tc.tile_pool(name="x_pool", bufs=N_GROUPS))
-        small = ctx.enter_context(tc.tile_pool(name="small", bufs=4))
-        xhat_pool = ctx.enter_context(tc.tile_pool(name="xhat_pool", bufs=3))
-        plane_pool = ctx.enter_context(tc.tile_pool(name="plane_pool", bufs=3))
+        small = ctx.enter_context(tc.tile_pool(name="small", bufs=6))
+        xhat_pool = ctx.enter_context(tc.tile_pool(name="xhat_pool", bufs=6))
+        plane_pool = ctx.enter_context(tc.tile_pool(name="plane_pool", bufs=6))
         row_pool = ctx.enter_context(tc.tile_pool(name="row_pool", bufs=2 * ROWS))
         stage_pool = ctx.enter_context(tc.tile_pool(name="stage_pool", bufs=3))
         turn_psum = ctx.enter_context(tc.psum_pool(name="turn_psum", bufs=2))
@@ -76,6 +73,8 @@ def tile_block_pa_t_kernel(tc, x, W_qkv, b_qkv, g1, beta1, out_0, out_1, out_2):
         w_sb = consts.tile([P, W_TILES, D], BF16)
         g1_in = consts.tile([P, PACK], BF16)
         beta1_in = consts.tile([P, PACK], BF16)
+        nc.scalar.dma_start(out=g1_in[:], in_=g1.rearrange("(p t) -> p t", t=PACK))
+        nc.scalar.dma_start(out=beta1_in[:], in_=beta1.rearrange("(p t) -> p t", t=PACK))
         bias = consts.tile([P, OUTS, D], BF16)
 
         def load_weights(o):
@@ -88,8 +87,6 @@ def tile_block_pa_t_kernel(tc, x, W_qkv, b_qkv, g1, beta1, out_0, out_1, out_2):
         nc.sync.dma_start(out=x_tiles[1][:], in_=x_groups[1])
         load_weights(1)
         load_weights(2)
-        nc.sync.dma_start(out=g1_in[:], in_=g1.rearrange("(p t) -> p t", t=PACK))
-        nc.sync.dma_start(out=beta1_in[:], in_=beta1.rearrange("(p t) -> p t", t=PACK))
         nc.sync.dma_start(out=x_tiles[2][:], in_=x_groups[2])
         nc.sync.dma_start(out=bias[:].rearrange("p o f -> p (o f)"), in_=b_qkv.partition_broadcast(P))
         for s in range(3, N_GROUPS):
@@ -143,120 +140,126 @@ def tile_block_pa_t_kernel(tc, x, W_qkv, b_qkv, g1, beta1, out_0, out_1, out_2):
         accs_of = {}
         stage_of = {}
 
-        def statistics(s, i):
-            if i == 0:
-                stats_of[s] = small.tile([P, ROWS, 6], F32, name="stats")
-            nc.vector.bn_stats(out=stats_of[s][:, i, :], in_=x_tiles[s][:, i, :])
+        def x_row(n):
+            return x_tiles[n // ROWS][:, n % ROWS, :]
 
-        def mean_and_rstd(s):
-            mean_var = small.tile([P, ROWS, 2], F32)
-            for i in range(ROWS):
-                nc.vector.bn_aggr(out=mean_var[:, i, :], in_=stats_of[s][:, i, :])
-            rstd = small.tile([P, ROWS], F32)
+        def statistics(n):
+            q, j = divmod(n, PAIR)
+            if j == 0:
+                stats_of[q] = small.tile([P, PAIR, 6], F32, name="stats")
+            nc.vector.bn_stats(out=stats_of[q][:, j, :], in_=x_row(n))
+
+        def mean_and_rstd(q):
+            mean_var = small.tile([P, PAIR, 2], F32)
+            for j in range(PAIR):
+                nc.vector.bn_aggr(out=mean_var[:, j, :], in_=stats_of[q][:, j, :])
+            rstd = small.tile([P, PAIR], F32)
             nc.scalar.activation(
                 out=rstd[:], in_=mean_var[:, :, 1], func=ACT.Abs_reciprocal_sqrt, bias=eps[:, 0:1], scale=1.0
             )
-            mean_var_of[s] = mean_var
-            rstd_of[s] = rstd
+            mean_var_of[q] = mean_var
+            rstd_of[q] = rstd
 
-        def shift(s):
-            shift_of[s] = small.tile([P, ROWS], F32, name="shift")
+        def shift(q):
+            shift_of[q] = small.tile([P, PAIR], F32, name="shift")
             nc.vector.scalar_tensor_tensor(
-                out=shift_of[s][:],
-                in0=mean_var_of[s][:, :, 0],
+                out=shift_of[q][:],
+                in0=mean_var_of[q][:, :, 0],
                 scalar=-1.0,
-                in1=rstd_of[s][:],
+                in1=rstd_of[q][:],
                 op0=ALU.mult,
                 op1=ALU.mult,
             )
 
-        def normalise_row(s, i):
-            if i == 0:
-                xhat_of[s] = xhat_pool.tile([P, ROWS, D], F32, name="xhat")
-            dst = xhat_of[s][:, i, :].rearrange("p (t q) -> p t q", t=PACK)
-            src = x_tiles[s][:, i, :].rearrange("p (q t) -> p t q", t=PACK)
-            engine = XHAT_ENGINES[0 if s == 0 else 1][i]
-            if engine == "scalar":
+        def normalise_row(n):
+            q, j = divmod(n, PAIR)
+            if j == 0:
+                xhat_of[q] = xhat_pool.tile([P, PAIR, D], F32, name="xhat")
+            dst = xhat_of[q][:, j, :].rearrange("p (t k) -> p t k", t=PACK)
+            src = x_row(n).rearrange("p (k t) -> p t k", t=PACK)
+            if j == 0 or n % XHAT_CYCLE == XHAT_CYCLE - 3:
+                nc.gpsimd.tensor_scalar(
+                    out=dst,
+                    in0=src,
+                    scalar1=rstd_of[q][:, j : j + 1],
+                    scalar2=shift_of[q][:, j : j + 1],
+                    op0=ALU.mult,
+                    op1=ALU.add,
+                )
+            else:
                 nc.scalar.activation(
                     out=dst,
                     in_=src,
                     func=ACT.Identity,
-                    scale=rstd_of[s][:, i : i + 1],
-                    bias=shift_of[s][:, i : i + 1],
-                )
-            else:
-                nc.gpsimd.tensor_scalar(
-                    out=dst,
-                    in0=src,
-                    scalar1=rstd_of[s][:, i : i + 1],
-                    scalar2=shift_of[s][:, i : i + 1],
-                    op0=ALU.mult,
-                    op1=ALU.add,
+                    scale=rstd_of[q][:, j : j + 1],
+                    bias=shift_of[q][:, j : j + 1],
                 )
 
-        def turn_plane(s, t):
-            plane = turn_psum.tile([P, GROUP], F32, tag="turn")
-            for i in range(ROWS):
-                nc.tensor.transpose(
-                    plane[:, i * P : (i + 1) * P], xhat_of[s][:, i, t * P : (t + 1) * P], ident_f32[:]
-                )
-            turned_of[s, t] = plane
+        def turn_step(q, half):
+            turned = turn_psum.tile([P, STEP_PLANES, PAIR * P], F32, tag="turn")
+            for c in range(STEP_PLANES):
+                t = half * STEP_PLANES + c
+                for j in range(PAIR):
+                    nc.tensor.transpose(
+                        turned[:, c, j * P : (j + 1) * P], xhat_of[q][:, j, t * P : (t + 1) * P], ident_f32[:]
+                    )
+            turned_of[q, half] = turned
 
-        def plane_out(s, t):
-            if t == 0:
-                planes_of[s] = plane_pool.tile([P, PACK, GROUP], BF16, name="planes")
-            nc.scalar.activation(
-                out=planes_of[s][:, t, :],
-                in_=turned_of[s, t][:],
-                func=ACT.Identity,
-                scale=affine[:, t : t + 1],
-                bias=affine[:, PACK + t : PACK + t + 1],
-            )
+        def planes_out(q, half):
+            if half == 0:
+                planes_of[q] = plane_pool.tile([P, PACK, PAIR * P], BF16, name="planes")
+            for c in range(STEP_PLANES):
+                t = half * STEP_PLANES + c
+                dst = planes_of[q][:, t, :]
+                src = turned_of[q, half][:, c, :]
+                gain = affine[:, t : t + 1]
+                offset = affine[:, PACK + t : PACK + t + 1]
+                nc.scalar.activation(out=dst, in_=src, func=ACT.Identity, scale=gain, bias=offset)
 
-        def regroup_row(s, i):
+        def regroup_row(n):
+            q, j = divmod(n, PAIR)
             grouped = row_pool.tile([P, P, PACK], BF16, align_bytes=64)
             nc.scalar.copy(
                 out=grouped[:].rearrange("p (c j) t -> p c t j", j=4),
-                in_=planes_of[s][:, :, i * P : (i + 1) * P].rearrange("p t (c j) -> p c t j", j=4),
+                in_=planes_of[q][:, :, j * P : (j + 1) * P].rearrange("p t (c j) -> p c t j", j=4),
             )
-            grouped_of[s, i] = grouped
+            grouped_of[n] = grouped
 
-        def quantise_row(s, i):
+        def quantise_row(n):
             codes = row_pool.tile([P, P], U32, align_bytes=64)
             scales = row_pool.tile([P, P], U8, align_bytes=64)
             nc.vector.quantize_mx(
                 out=codes[:].bitcast(FP8X4),
                 scales=scales[:],
-                in_=grouped_of[s, i][:].rearrange("p c t -> p (c t)"),
+                in_=grouped_of[n][:].rearrange("p c t -> p (c t)"),
             )
-            codes_of[s, i] = codes
-            scales_of[s, i] = scales
+            codes_of[n] = codes
+            scales_of[n] = scales
 
-        def matmul_row(s, i):
+        def matmul_row(n):
             accs = []
             for o in range(OUTS):
                 acc = acc_psum.tile([P, D], F32, name="acc_%d" % o)
                 nc.tensor.matmul_mx(
                     out=acc[:],
-                    lhsT=codes_of[s, i][:].bitcast(FP8X4),
-                    lhsT_scale=scales_of[s, i][:],
+                    lhsT=codes_of[n][:].bitcast(FP8X4),
+                    lhsT_scale=scales_of[n][:],
                     rhs=w_codes[:, o * D : (o + 1) * D].bitcast(FP8X4),
                     rhs_scale=w_scales[:, o * D : (o + 1) * D],
                     start=True,
                     stop=True,
                 )
                 accs.append(acc)
-            accs_of[s, i] = accs
+            accs_of[n] = accs
 
-        def bias_row(s, i):
+        def bias_row(n):
+            s, i = divmod(n, ROWS)
             if i == 0:
                 stage_of[s] = [
                     stage_pool.tile([P, ROWS, D], F32, name="stage_%d" % o) for o in range(OUTS)
                 ]
-            accs = accs_of[s, i]
-            row = s * ROWS + i
-            after = row - FIRST_ROW_AFTER_STATISTICS
-            vector_takes_v = (after >= 0 and after % 2 == 0) or row == N_ROWS - 1
+            accs = accs_of[n]
+            vector_takes_v = n % VECTOR_V_ROWS == VECTOR_V_ROWS - 2 or n == N_ROWS - 1
             for o in range(OUTS):
                 dst = stage_of[s][o][:, i, :]
                 if o < OUTS - 1 or vector_takes_v:
@@ -269,43 +272,37 @@ def tile_block_pa_t_kernel(tc, x, W_qkv, b_qkv, g1, beta1, out_0, out_1, out_2):
                 for o in range(OUTS):
                     nc.sync.dma_start(out=out_groups[o][s][:, done, :], in_=stage_of[s][o][:, done, :])
 
+        def row_at(step, lag):
+            return [step - lag] if 0 <= step - lag < N_ROWS else []
+
         for step in range(N_STEPS):
-            n = step - LAG_RSTD
-            group_is_counted = n % ROWS == 0 and 0 <= n < N_ROWS
-            if group_is_counted:
-                mean_and_rstd(n // ROWS)
-            n = step - LAG_MATMUL
-            if 0 <= n < N_ROWS:
-                matmul_row(n // ROWS, n % ROWS)
-            n = step - LAG_XHAT
-            if 0 <= n < N_ROWS and n % ROWS < ROWS // XHAT_ROWS:
-                for i in range(n % ROWS * XHAT_ROWS, (n % ROWS + 1) * XHAT_ROWS):
-                    normalise_row(n // ROWS, i)
-            o = step - W_QUANTISE_STEP
-            if 0 <= o < OUTS:
-                quantise_weights(o)
-            n = step - LAG_BIAS
-            if 0 <= n < N_ROWS:
-                bias_row(n // ROWS, n % ROWS)
-            if step < N_ROWS:
-                statistics(step // ROWS, step % ROWS)
+            counted = [n // PAIR for n in row_at(step, LAG_RSTD) if n % PAIR == 0]
+            for q in counted:
+                mean_and_rstd(q)
+            for n in row_at(step, LAG_XHAT):
+                normalise_row(n)
+            for n in row_at(step, LAG_BIAS):
+                bias_row(n)
+            for n in row_at(step, 0):
+                statistics(n)
+            if step == LAG_PLANE_OUT - 1:
+                widen_affine()
+            for n in row_at(step, LAG_PLANE_OUT):
+                planes_out(n // PAIR, n % PAIR)
+            for n in row_at(step, LAG_QUANTISE):
+                quantise_row(n)
             w = (step - W_FIRST_STEP) * W_STEP_TILES
             if 0 <= w < W_TILES:
                 for r in range(w, w + W_STEP_TILES):
                     turn_weight_tile(r)
-            if step == LAG_TURN - 1:
-                widen_affine()
-            n = step - LAG_TURN
-            if 0 <= n < N_ROWS:
-                turn_plane(n // PACK, n % PACK)
-            n = step - LAG_PLANE_OUT
-            if 0 <= n < N_ROWS:
-                plane_out(n // PACK, n % PACK)
-            if group_is_counted:
-                shift((step - LAG_RSTD) // ROWS)
-            n = step - LAG_QUANTISE
-            if 0 <= n < N_ROWS:
-                quantise_row(n // ROWS, n % ROWS)
-            n = step - LAG_REGROUP
-            if 0 <= n < N_ROWS:
-                regroup_row(n // ROWS, n % ROWS)
+            o = step - W_QUANTISE_STEP
+            if 0 <= o < OUTS:
+                quantise_weights(o)
+            for n in row_at(step, LAG_REGROUP):
+                regroup_row(n)
+            for n in row_at(step, LAG_MATMUL):
+                matmul_row(n)
+            for n in row_at(step, LAG_TURN):
+                turn_step(n // PAIR, n % PAIR)
+            for q in counted:
+                shift(q)

from contextlib import ExitStack

import concourse.mybir as mybir
from concourse.masks import make_identity

F32 = mybir.dt.float32
BF16 = mybir.dt.bfloat16
U32 = mybir.dt.uint32
U8 = mybir.dt.uint8
FP8X4 = mybir.dt.float8_e4m3fn_x4
ACT = mybir.ActivationFunctionType
ALU = mybir.AluOpType

P = 128
PACK = 4
HALVES = 2
D = P * PACK
TOKENS = 4 * 1024
OUTS = 3
ROWS = 4
PAIR = 2
GROUP = P * ROWS
N_GROUPS = TOKENS // GROUP
N_ROWS = N_GROUPS * ROWS
W_TILES = OUTS * D // P
W_STEP_TILES = 2
W_FIRST_STEP = 2
W_QUANTISE_STEP = 6
LN_EPS = 1e-6

LAG_RSTD = PAIR
LAG_XHAT = LAG_RSTD + 1
LAG_TURN = LAG_XHAT + PAIR
STEP_PLANES = PACK // PAIR
LAG_PLANE_OUT = LAG_TURN + 1
LAG_REGROUP = LAG_PLANE_OUT + PAIR - 1
LAG_QUANTISE = LAG_REGROUP + 1
LAG_MATMUL = LAG_QUANTISE + 1
LAG_BIAS = LAG_MATMUL + 1
N_STEPS = N_ROWS + LAG_BIAS
STORE_ROWS = 2
XHAT_CYCLE = 8
VECTOR_V_ROWS = 5

FLOPS = 2 * TOKENS * D * OUTS * D


def tile_block_pa_t_kernel(tc, x, W_qkv, b_qkv, g1, beta1, out_0, out_1, out_2):
    nc = tc.nc

    x_groups = x.flatten_outer_dims().rearrange("(s p i) k -> s p i k", p=P, i=ROWS)
    out_groups = [
        out.rearrange("b t h d -> (b t) (h d)").rearrange("(s p i) f -> s p i f", p=P, i=ROWS)
        for out in (out_0, out_1, out_2)
    ]
    w_rows = W_qkv.rearrange("(r p) k -> p r k", p=P)

    with ExitStack() as ctx:
        consts = ctx.enter_context(tc.tile_pool(name="consts", bufs=1))
        x_pool = ctx.enter_context(tc.tile_pool(name="x_pool", bufs=N_GROUPS))
        small = ctx.enter_context(tc.tile_pool(name="small", bufs=6))
        xhat_pool = ctx.enter_context(tc.tile_pool(name="xhat_pool", bufs=6))
        plane_pool = ctx.enter_context(tc.tile_pool(name="plane_pool", bufs=6))
        row_pool = ctx.enter_context(tc.tile_pool(name="row_pool", bufs=2 * ROWS))
        stage_pool = ctx.enter_context(tc.tile_pool(name="stage_pool", bufs=3))
        turn_psum = ctx.enter_context(tc.psum_pool(name="turn_psum", bufs=2))
        acc_psum = ctx.enter_context(tc.psum_pool(name="acc_psum", bufs=2))
        ctx.enter_context(tc.manual_schedule())

        x_tiles = []
        for s in range(N_GROUPS):
            x_tiles.append(x_pool.tile([P, ROWS, D], BF16, name="x_grp", tag="x_grp"))
        w_sb = consts.tile([P, W_TILES, D], BF16)
        g1_in = consts.tile([P, PACK], BF16)
        beta1_in = consts.tile([P, PACK], BF16)
        nc.scalar.dma_start(out=g1_in[:], in_=g1.rearrange("(p t) -> p t", t=PACK))
        nc.scalar.dma_start(out=beta1_in[:], in_=beta1.rearrange("(p t) -> p t", t=PACK))
        bias = consts.tile([P, OUTS, D], BF16)

        def load_weights(o):
            tiles_of_o = slice(o * PACK, (o + 1) * PACK)
            nc.sync.dma_start(out=w_sb[:, tiles_of_o, :], in_=w_rows[:, tiles_of_o, :])

        for half in (slice(0, ROWS // 2), slice(ROWS // 2, ROWS)):
            nc.sync.dma_start(out=x_tiles[0][:, half, :], in_=x_groups[0][:, half, :])
        load_weights(0)
        nc.sync.dma_start(out=x_tiles[1][:], in_=x_groups[1])
        load_weights(1)
        load_weights(2)
        nc.sync.dma_start(out=x_tiles[2][:], in_=x_groups[2])
        nc.sync.dma_start(out=bias[:].rearrange("p o f -> p (o f)"), in_=b_qkv.partition_broadcast(P))
        for s in range(3, N_GROUPS):
            nc.sync.dma_start(out=x_tiles[s][:], in_=x_groups[s])

        ident_f32 = consts.tile([P, P], F32)
        make_identity(nc, ident_f32[:])
        eps = consts.tile([P, 1], F32)
        nc.vector.memset(eps[:], LN_EPS)
        warm = consts.tile([P, 1], F32)
        nc.scalar.activation(out=warm[:], in_=eps[:], func=ACT.Abs_reciprocal_sqrt)

        affine = consts.tile([P, 2 * PACK], F32)

        def widen_affine():
            nc.vector.tensor_copy(out=affine[:, 0:PACK], in_=g1_in[:])
            nc.vector.tensor_copy(out=affine[:, PACK : 2 * PACK], in_=beta1_in[:])

        w_words = w_sb[:].bitcast(F32)
        w_grouped = consts.tile([P, OUTS * D, PACK], BF16, align_bytes=64)
        w_grouped_words = w_grouped[:].bitcast(F32)
        w_codes = consts.tile([P, OUTS * D], U32, align_bytes=64)
        w_scales = consts.tile([P, OUTS * D], U8, align_bytes=64)

        def turn_weight_tile(r):
            w_turned = acc_psum.tile([P, HALVES, P], F32, tag="acc_%d" % (r % OUTS))
            for u in range(HALVES):
                nc.tensor.transpose(w_turned[:, u, :], w_words[:, r, u::HALVES], ident_f32[:])
            nc.scalar.copy(
                out=w_grouped_words[:, r * P : (r + 1) * P, :], in_=w_turned[:].rearrange("p u f -> p f u")
            )

        def quantise_weights(o):
            cols = slice(o * D, (o + 1) * D)
            nc.vector.quantize_mx(
                out=w_codes[:, cols].bitcast(FP8X4),
                scales=w_scales[:, cols],
                in_=w_grouped[:, cols, :].rearrange("p f t -> p (f t)"),
            )

        stats_of = {}
        mean_var_of = {}
        rstd_of = {}
        shift_of = {}
        xhat_of = {}
        turned_of = {}
        planes_of = {}
        grouped_of = {}
        codes_of = {}
        scales_of = {}
        accs_of = {}
        stage_of = {}

        def x_row(n):
            return x_tiles[n // ROWS][:, n % ROWS, :]

        def statistics(n):
            q, j = divmod(n, PAIR)
            if j == 0:
                stats_of[q] = small.tile([P, PAIR, 6], F32, name="stats")
            nc.vector.bn_stats(out=stats_of[q][:, j, :], in_=x_row(n))

        def mean_and_rstd(q):
            mean_var = small.tile([P, PAIR, 2], F32)
            for j in range(PAIR):
                nc.vector.bn_aggr(out=mean_var[:, j, :], in_=stats_of[q][:, j, :])
            rstd = small.tile([P, PAIR], F32)
            nc.scalar.activation(
                out=rstd[:], in_=mean_var[:, :, 1], func=ACT.Abs_reciprocal_sqrt, bias=eps[:, 0:1], scale=1.0
            )
            mean_var_of[q] = mean_var
            rstd_of[q] = rstd

        def shift(q):
            shift_of[q] = small.tile([P, PAIR], F32, name="shift")
            nc.vector.scalar_tensor_tensor(
                out=shift_of[q][:],
                in0=mean_var_of[q][:, :, 0],
                scalar=-1.0,
                in1=rstd_of[q][:],
                op0=ALU.mult,
                op1=ALU.mult,
            )

        def normalise_row(n):
            q, j = divmod(n, PAIR)
            if j == 0:
                xhat_of[q] = xhat_pool.tile([P, PAIR, D], F32, name="xhat")
            dst = xhat_of[q][:, j, :].rearrange("p (t k) -> p t k", t=PACK)
            src = x_row(n).rearrange("p (k t) -> p t k", t=PACK)
            if j == 0 or n % XHAT_CYCLE == XHAT_CYCLE - 3:
                nc.gpsimd.tensor_scalar(
                    out=dst,
                    in0=src,
                    scalar1=rstd_of[q][:, j : j + 1],
                    scalar2=shift_of[q][:, j : j + 1],
                    op0=ALU.mult,
                    op1=ALU.add,
                )
            else:
                nc.scalar.activation(
                    out=dst,
                    in_=src,
                    func=ACT.Identity,
                    scale=rstd_of[q][:, j : j + 1],
                    bias=shift_of[q][:, j : j + 1],
                )

        def turn_step(q, half):
            turned = turn_psum.tile([P, STEP_PLANES, PAIR * P], F32, tag="turn")
            for c in range(STEP_PLANES):
                t = half * STEP_PLANES + c
                for j in range(PAIR):
                    nc.tensor.transpose(
                        turned[:, c, j * P : (j + 1) * P], xhat_of[q][:, j, t * P : (t + 1) * P], ident_f32[:]
                    )
            turned_of[q, half] = turned

        def planes_out(q, half):
            if half == 0:
                planes_of[q] = plane_pool.tile([P, PACK, PAIR * P], BF16, name="planes")
            for c in range(STEP_PLANES):
                t = half * STEP_PLANES + c
                dst = planes_of[q][:, t, :]
                src = turned_of[q, half][:, c, :]
                gain = affine[:, t : t + 1]
                offset = affine[:, PACK + t : PACK + t + 1]
                nc.scalar.activation(out=dst, in_=src, func=ACT.Identity, scale=gain, bias=offset)

        def regroup_row(n):
            q, j = divmod(n, PAIR)
            grouped = row_pool.tile([P, P, PACK], BF16, align_bytes=64)
            nc.scalar.copy(
                out=grouped[:].rearrange("p (c j) t -> p c t j", j=4),
                in_=planes_of[q][:, :, j * P : (j + 1) * P].rearrange("p t (c j) -> p c t j", j=4),
            )
            grouped_of[n] = grouped

        def quantise_row(n):
            codes = row_pool.tile([P, P], U32, align_bytes=64)
            scales = row_pool.tile([P, P], U8, align_bytes=64)
            nc.vector.quantize_mx(
                out=codes[:].bitcast(FP8X4),
                scales=scales[:],
                in_=grouped_of[n][:].rearrange("p c t -> p (c t)"),
            )
            codes_of[n] = codes
            scales_of[n] = scales

        def matmul_row(n):
            accs = []
            for o in range(OUTS):
                acc = acc_psum.tile([P, D], F32, name="acc_%d" % o)
                nc.tensor.matmul_mx(
                    out=acc[:],
                    lhsT=codes_of[n][:].bitcast(FP8X4),
                    lhsT_scale=scales_of[n][:],
                    rhs=w_codes[:, o * D : (o + 1) * D].bitcast(FP8X4),
                    rhs_scale=w_scales[:, o * D : (o + 1) * D],
                    start=True,
                    stop=True,
                )
                accs.append(acc)
            accs_of[n] = accs

        def bias_row(n):
            s, i = divmod(n, ROWS)
            if i == 0:
                stage_of[s] = [
                    stage_pool.tile([P, ROWS, D], F32, name="stage_%d" % o) for o in range(OUTS)
                ]
            accs = accs_of[n]
            vector_takes_v = n % VECTOR_V_ROWS == VECTOR_V_ROWS - 2 or n == N_ROWS - 1
            for o in range(OUTS):
                dst = stage_of[s][o][:, i, :]
                if o < OUTS - 1 or vector_takes_v:
                    nc.vector.tensor_tensor(out=dst, in0=accs[o][:], in1=bias[:, o, :], op=ALU.add)
                else:
                    nc.scalar.copy(out=dst, in_=accs[o][:])
                    nc.gpsimd.tensor_tensor(out=dst, in0=dst, in1=bias[:, o, :], op=ALU.add)
            if (i + 1) % STORE_ROWS == 0:
                done = slice(i + 1 - STORE_ROWS, i + 1)
                for o in range(OUTS):
                    nc.sync.dma_start(out=out_groups[o][s][:, done, :], in_=stage_of[s][o][:, done, :])

        def row_at(step, lag):
            return [step - lag] if 0 <= step - lag < N_ROWS else []

        for step in range(N_STEPS):
            counted = [n // PAIR for n in row_at(step, LAG_RSTD) if n % PAIR == 0]
            for q in counted:
                mean_and_rstd(q)
            for n in row_at(step, LAG_XHAT):
                normalise_row(n)
            for n in row_at(step, LAG_BIAS):
                bias_row(n)
            for n in row_at(step, 0):
                statistics(n)
            if step == LAG_PLANE_OUT - 1:
                widen_affine()
            for n in row_at(step, LAG_PLANE_OUT):
                planes_out(n // PAIR, n % PAIR)
            for n in row_at(step, LAG_QUANTISE):
                quantise_row(n)
            w = (step - W_FIRST_STEP) * W_STEP_TILES
            if 0 <= w < W_TILES:
                for r in range(w, w + W_STEP_TILES):
                    turn_weight_tile(r)
            o = step - W_QUANTISE_STEP
            if 0 <= o < OUTS:
                quantise_weights(o)
            for n in row_at(step, LAG_REGROUP):
                regroup_row(n)
            for n in row_at(step, LAG_MATMUL):
                matmul_row(n)
            for n in row_at(step, LAG_TURN):
                turn_step(n // PAIR, n % PAIR)
            for q in counted:
                shift(q)
